import numpy as np
import ml_dtypes


def mxq(x, axis, fmt="e4m3"):
    dtype, down = {"e4m3": (ml_dtypes.float8_e4m3fn, 7), "e5m2": (ml_dtypes.float8_e5m2, 14)}[fmt]
    v = np.moveaxis(np.asarray(x, np.float32).astype(ml_dtypes.bfloat16).astype(np.float64), axis, -1)
    blocks = v.reshape(v.shape[:-1] + (-1, 32))
    amax = np.abs(blocks).max(-1, keepdims=True)
    byte = np.maximum(np.where(amax > 0, np.frexp(amax)[1] - 1 + 127, 0) - down, 1)
    scale = np.exp2(byte - 127.0)
    codes = (blocks / scale).astype(np.float32).astype(dtype).astype(np.float64)
    return np.moveaxis((codes * scale).reshape(v.shape), -1, axis)


BF16 = ml_dtypes.bfloat16


def bf(x):
    return np.asarray(x, np.float32).astype(BF16)


def f64(x):
    return np.asarray(x).astype(np.float64)


B, K, N = 8192, 512, 256


def binarize(v):
    return np.where(v >= 0, 1.0, -1.0)


def setup_inputs():
    return {"x": bf(np.random.standard_normal((B, K)) * 3.0 / np.sqrt(K)),
            "w": bf(np.random.standard_normal((K, N)) * 0.6)}


def reference(x, w):
    w_c = np.clip(f64(w), -1.0, 1.0)
    w_b = binarize(w_c)
    return mxq(f64(x), 1, "e4m3") @ mxq(w_b, 0, "e4m3")

@@ -1,0 +1,159 @@
+from contextlib import ExitStack
+
+import concourse.mybir as mybir
+from concourse.masks import make_identity
+
+F32 = mybir.dt.float32
+BF16 = mybir.dt.bfloat16
+U32 = mybir.dt.uint32
+U8 = mybir.dt.uint8
+FP8X4 = mybir.dt.float8_e4m3fn_x4
+ALU = mybir.AluOpType
+
+P = 128
+B, K, N = 8192, 512, 256
+TILES = B // P
+KW = K // 2
+
+FLOPS = 2 * B * K * N
+
+ROUNDS = [4, 4, 8, 8, 8, 8, 8, 8, 8]
+LOADS = [4, 4, 8, 16, 16, 16]
+STORES = [16, 16, 16, 8, 8]
+
+
+def tile_binlinear_t_kernel(tc, x, w, out):
+    nc = tc.nc
+    x_rows = x.rearrange("(p t) k -> p (t k)", t=TILES)
+    out_rows = out.rearrange("(p t) n -> p (t n)", t=TILES)
+
+    with ExitStack() as ctx:
+        keep = ctx.enter_context(tc.tile_pool(name="keep", bufs=1))
+        ring = ctx.enter_context(tc.tile_pool(name="ring", bufs=3))
+        psum_x = ctx.enter_context(tc.psum_pool(name="psum_x", bufs=4))
+        psum_o = ctx.enter_context(tc.psum_pool(name="psum_o", bufs=4))
+        ctx.enter_context(tc.manual_schedule())
+
+        w_raw = keep.tile([P, 4 * N], BF16, name="w_raw")
+        nc.sync.dma_start(
+            out=w_raw[:].rearrange("p (u e n) -> p u e n", u=2, e=2),
+            in_=w.rearrange("(u p e) n -> p u e n", u=2, e=2),
+        )
+        x_words = []
+        first = 0
+        for c, size in enumerate(LOADS):
+            x_chunk = keep.tile([P, size * K], BF16, name="x%d" % c)
+            nc.sync.dma_start(out=x_chunk[:], in_=x_rows[:, first * K : (first + size) * K])
+            words = x_chunk[:].bitcast(F32)
+            for i in range(size):
+                x_words.append(words[:, i * KW : (i + 1) * KW])
+            first += size
+
+        ident = keep.tile([P, P], F32, name="ident")
+        make_identity(nc, ident[:])
+
+        out_banks = []
+        store_after = {}
+        first = 0
+        for c, size in enumerate(STORES):
+            out_chunk = keep.tile([P, size * N], F32, name="o%d" % c)
+            for i in range(size // 2):
+                out_banks.append(out_chunk[:, i * 2 * N : (i + 1) * 2 * N])
+            store_after[(first + size) // 2 - 1] = (out_chunk, first, size)
+            first += size
+
+        w_clip = keep.tile([P, 4 * N], BF16, name="w_clip")
+        nc.vector.tensor_scalar(
+            out=w_clip[:], in0=w_raw[:], scalar1=-1.0, scalar2=1.0, op0=ALU.max, op1=ALU.min
+        )
+        w_step = keep.tile([P, 4 * N], BF16, name="w_step")
+        nc.vector.tensor_scalar(
+            out=w_step[:], in0=w_clip[:], scalar1=0.0, scalar2=2.0, op0=ALU.is_ge, op1=ALU.mult
+        )
+        w_bin = keep.tile([P, 4 * N], BF16, name="w_bin", align_bytes=64)
+        nc.vector.tensor_scalar(
+            out=w_bin[:].rearrange("p (n t) -> p n t", t=4),
+            in0=w_step[:].rearrange("p (t n) -> p n t", t=4),
+            scalar1=-1.0,
+            scalar2=None,
+            op0=ALU.add,
+        )
+        w_codes = keep.tile([P, N], U32, name="w_codes", align_bytes=64)
+        w_scales = keep.tile([P, N], U8, name="w_scales", align_bytes=64)
+
+        def transpose_round(first_tile, size):
+            banks = []
+            for b in range(size // 2):
+                xt = psum_x.tile([P, 2, 2, P], F32, name="xt")
+                for j in range(2):
+                    for u in range(2):
+                        nc.tensor.transpose(
+                            xt[:, j, u, :],
+                            x_words[first_tile + 2 * b + j][:, u * P : (u + 1) * P],
+                            ident[:],
+                        )
+                banks.append(xt)
+            return banks
+
+        def regroup_round(first_tile, size, banks):
+            grouped = ring.tile([P, size * K], BF16, name="grouped", tag="grouped", align_bytes=64)
+            grouped_words = grouped[:].bitcast(F32)
+            for b, xt in enumerate(banks):
+                dst = grouped_words[:, b * 2 * KW : (b + 1) * 2 * KW].rearrange(
+                    "p (j r u) -> p j r u", j=2, u=2
+                )
+                src = xt[:].rearrange("p j u r -> p j r u")
+                if (first_tile // 2 + b) % 2 == 0:
+                    nc.vector.tensor_copy(out=dst, in_=src)
+                else:
+                    nc.scalar.copy(out=dst, in_=src)
+            return grouped
+
+        def quantise_round(size, grouped):
+            codes = ring.tile([P, size * P], U32, name="codes", tag="codes", align_bytes=64)
+            scales = ring.tile([P, size * P], U8, name="scales", tag="scales", align_bytes=64)
+            nc.vector.quantize_mx(out=codes[:].bitcast(FP8X4), scales=scales[:], in_=grouped[:])
+            return codes, scales
+
+        def multiply_round(first_tile, size, codes, scales, last):
+            banks = []
+            for b in range(size // 2):
+                acc = psum_o.tile([P, 2, N], F32, name="acc")
+                for j in range(2):
+                    cols = slice((2 * b + j) * P, (2 * b + j + 1) * P)
+                    nc.tensor.matmul_mx(
+                        out=acc[:, j, :],
+                        lhsT=codes[:, cols].bitcast(FP8X4),
+                        lhsT_scale=scales[:, cols],
+                        rhs=w_codes[:].bitcast(FP8X4),
+                        rhs_scale=w_scales[:],
+                        start=True,
+                        stop=True,
+                    )
+                banks.append(acc)
+            for b, acc in enumerate(banks):
+                g = first_tile // 2 + b
+                src = acc[:].rearrange("p j n -> p (j n)")
+                on_vector = (g % 2 == 0) if last else (g % 4 == 0)
+                if on_vector:
+                    nc.vector.tensor_copy(out=out_banks[g], in_=src)
+                else:
+                    nc.scalar.copy(out=out_banks[g], in_=src)
+                if g in store_after:
+                    out_chunk, t0, n_tiles = store_after[g]
+                    nc.sync.dma_start(
+                        out=out_rows[:, t0 * N : (t0 + n_tiles) * N], in_=out_chunk[:]
+                    )
+
+        starts = [sum(ROUNDS[:s]) for s in range(len(ROUNDS))]
+        n_rounds = len(ROUNDS)
+
+        banks = transpose_round(starts[0], ROUNDS[0])
+        grouped = regroup_round(starts[0], ROUNDS[0], banks)
+        nc.vector.quantize_mx(out=w_codes[:].bitcast(FP8X4), scales=w_scales[:], in_=w_bin[:])
+        for s in range(1, n_rounds + 1):
+            codes, scales = quantise_round(ROUNDS[s - 1], grouped)
+            if s < n_rounds:
+                banks = transpose_round(starts[s], ROUNDS[s])
+                grouped = regroup_round(starts[s], ROUNDS[s], banks)
+            multiply_round(starts[s - 1], ROUNDS[s - 1], codes, scales, s == n_rounds)

@@ -17,9 +17,9 @@ KW = K // 2
 
 FLOPS = 2 * B * K * N
 
-ROUNDS = [4, 4, 8, 8, 8, 8, 8, 8, 8]
-LOADS = [4, 4, 8, 16, 16, 16]
-STORES = [16, 16, 16, 8, 8]
+ROUNDS = [4, 4, 8, 8, 8, 8, 8, 8, 4, 4]
+LOADS = [4, 4, 8, 8, 8, 8, 8, 16]
+STORES = [16, 16, 8, 8, 8, 4, 4]
 
 
 def tile_binlinear_t_kernel(tc, x, w, out):

@@ -17,9 +17,9 @@ KW = K // 2
 
 FLOPS = 2 * B * K * N
 
-ROUNDS = [4, 4, 8, 8, 8, 8, 8, 8, 4, 4]
-LOADS = [4, 4, 8, 8, 8, 8, 8, 16]
-STORES = [16, 16, 8, 8, 8, 4, 4]
+ROUNDS = [4, 4, 8, 8, 8, 8, 8, 8, 4, 2, 2]
+LOADS = [4, 4, 8, 8, 8, 16, 16]
+STORES = [16, 16, 8, 8, 8, 4, 2, 2]
 
 
 def tile_binlinear_t_kernel(tc, x, w, out):

@@ -17,9 +17,9 @@ KW = K // 2
 
 FLOPS = 2 * B * K * N
 
-ROUNDS = [4, 4, 8, 8, 8, 8, 8, 8, 4, 2, 2]
+ROUNDS = [4, 4, 8, 8, 8, 8, 8, 8, 8]
 LOADS = [4, 4, 8, 8, 8, 16, 16]
-STORES = [16, 16, 8, 8, 8, 4, 2, 2]
+STORES = [24, 16, 8, 8, 8]
 
 
 def tile_binlinear_t_kernel(tc, x, w, out):

from contextlib import ExitStack

import concourse.mybir as mybir
from concourse.masks import make_identity

F32 = mybir.dt.float32
BF16 = mybir.dt.bfloat16
U32 = mybir.dt.uint32
U8 = mybir.dt.uint8
FP8X4 = mybir.dt.float8_e4m3fn_x4
ALU = mybir.AluOpType

P = 128
B, K, N = 8192, 512, 256
TILES = B // P
KW = K // 2

FLOPS = 2 * B * K * N

ROUNDS = [4, 4, 8, 8, 8, 8, 8, 8, 8]
LOADS = [4, 4, 8, 8, 8, 16, 16]
STORES = [24, 16, 8, 8, 8]


def tile_binlinear_t_kernel(tc, x, w, out):
    nc = tc.nc
    x_rows = x.rearrange("(p t) k -> p (t k)", t=TILES)
    out_rows = out.rearrange("(p t) n -> p (t n)", t=TILES)

    with ExitStack() as ctx:
        keep = ctx.enter_context(tc.tile_pool(name="keep", bufs=1))
        ring = ctx.enter_context(tc.tile_pool(name="ring", bufs=3))
        psum_x = ctx.enter_context(tc.psum_pool(name="psum_x", bufs=4))
        psum_o = ctx.enter_context(tc.psum_pool(name="psum_o", bufs=4))
        ctx.enter_context(tc.manual_schedule())

        w_raw = keep.tile([P, 4 * N], BF16, name="w_raw")
        nc.sync.dma_start(
            out=w_raw[:].rearrange("p (u e n) -> p u e n", u=2, e=2),
            in_=w.rearrange("(u p e) n -> p u e n", u=2, e=2),
        )
        x_words = []
        first = 0
        for c, size in enumerate(LOADS):
            x_chunk = keep.tile([P, size * K], BF16, name="x%d" % c)
            nc.sync.dma_start(out=x_chunk[:], in_=x_rows[:, first * K : (first + size) * K])
            words = x_chunk[:].bitcast(F32)
            for i in range(size):
                x_words.append(words[:, i * KW : (i + 1) * KW])
            first += size

        ident = keep.tile([P, P], F32, name="ident")
        make_identity(nc, ident[:])

        out_banks = []
        store_after = {}
        first = 0
        for c, size in enumerate(STORES):
            out_chunk = keep.tile([P, size * N], F32, name="o%d" % c)
            for i in range(size // 2):
                out_banks.append(out_chunk[:, i * 2 * N : (i + 1) * 2 * N])
            store_after[(first + size) // 2 - 1] = (out_chunk, first, size)
            first += size

        w_clip = keep.tile([P, 4 * N], BF16, name="w_clip")
        nc.vector.tensor_scalar(
            out=w_clip[:], in0=w_raw[:], scalar1=-1.0, scalar2=1.0, op0=ALU.max, op1=ALU.min
        )
        w_step = keep.tile([P, 4 * N], BF16, name="w_step")
        nc.vector.tensor_scalar(
            out=w_step[:], in0=w_clip[:], scalar1=0.0, scalar2=2.0, op0=ALU.is_ge, op1=ALU.mult
        )
        w_bin = keep.tile([P, 4 * N], BF16, name="w_bin", align_bytes=64)
        nc.vector.tensor_scalar(
            out=w_bin[:].rearrange("p (n t) -> p n t", t=4),
            in0=w_step[:].rearrange("p (t n) -> p n t", t=4),
            scalar1=-1.0,
            scalar2=None,
            op0=ALU.add,
        )
        w_codes = keep.tile([P, N], U32, name="w_codes", align_bytes=64)
        w_scales = keep.tile([P, N], U8, name="w_scales", align_bytes=64)

        def transpose_round(first_tile, size):
            banks = []
            for b in range(size // 2):
                xt = psum_x.tile([P, 2, 2, P], F32, name="xt")
                for j in range(2):
                    for u in range(2):
                        nc.tensor.transpose(
                            xt[:, j, u, :],
                            x_words[first_tile + 2 * b + j][:, u * P : (u + 1) * P],
                            ident[:],
                        )
                banks.append(xt)
            return banks

        def regroup_round(first_tile, size, banks):
            grouped = ring.tile([P, size * K], BF16, name="grouped", tag="grouped", align_bytes=64)
            grouped_words = grouped[:].bitcast(F32)
            for b, xt in enumerate(banks):
                dst = grouped_words[:, b * 2 * KW : (b + 1) * 2 * KW].rearrange(
                    "p (j r u) -> p j r u", j=2, u=2
                )
                src = xt[:].rearrange("p j u r -> p j r u")
                if (first_tile // 2 + b) % 2 == 0:
                    nc.vector.tensor_copy(out=dst, in_=src)
                else:
                    nc.scalar.copy(out=dst, in_=src)
            return grouped

        def quantise_round(size, grouped):
            codes = ring.tile([P, size * P], U32, name="codes", tag="codes", align_bytes=64)
            scales = ring.tile([P, size * P], U8, name="scales", tag="scales", align_bytes=64)
            nc.vector.quantize_mx(out=codes[:].bitcast(FP8X4), scales=scales[:], in_=grouped[:])
            return codes, scales

        def multiply_round(first_tile, size, codes, scales, last):
            banks = []
            for b in range(size // 2):
                acc = psum_o.tile([P, 2, N], F32, name="acc")
                for j in range(2):
                    cols = slice((2 * b + j) * P, (2 * b + j + 1) * P)
                    nc.tensor.matmul_mx(
                        out=acc[:, j, :],
                        lhsT=codes[:, cols].bitcast(FP8X4),
                        lhsT_scale=scales[:, cols],
                        rhs=w_codes[:].bitcast(FP8X4),
                        rhs_scale=w_scales[:],
                        start=True,
                        stop=True,
                    )
                banks.append(acc)
            for b, acc in enumerate(banks):
                g = first_tile // 2 + b
                src = acc[:].rearrange("p j n -> p (j n)")
                on_vector = (g % 2 == 0) if last else (g % 4 == 0)
                if on_vector:
                    nc.vector.tensor_copy(out=out_banks[g], in_=src)
                else:
                    nc.scalar.copy(out=out_banks[g], in_=src)
                if g in store_after:
                    out_chunk, t0, n_tiles = store_after[g]
                    nc.sync.dma_start(
                        out=out_rows[:, t0 * N : (t0 + n_tiles) * N], in_=out_chunk[:]
                    )

        starts = [sum(ROUNDS[:s]) for s in range(len(ROUNDS))]
        n_rounds = len(ROUNDS)

        banks = transpose_round(starts[0], ROUNDS[0])
        grouped = regroup_round(starts[0], ROUNDS[0], banks)
        nc.vector.quantize_mx(out=w_codes[:].bitcast(FP8X4), scales=w_scales[:], in_=w_bin[:])
        for s in range(1, n_rounds + 1):
            codes, scales = quantise_round(ROUNDS[s - 1], grouped)
            if s < n_rounds:
                banks = transpose_round(starts[s], ROUNDS[s])
                grouped = regroup_round(starts[s], ROUNDS[s], banks)
            multiply_round(starts[s - 1], ROUNDS[s - 1], codes, scales, s == n_rounds)
